import numpy as np
import ml_dtypes


def mxq(x, axis, fmt="e4m3"):
    dtype, down = {"e4m3": (ml_dtypes.float8_e4m3fn, 7), "e5m2": (ml_dtypes.float8_e5m2, 14)}[fmt]
    v = np.moveaxis(np.asarray(x, np.float32).astype(ml_dtypes.bfloat16).astype(np.float64), axis, -1)
    blocks = v.reshape(v.shape[:-1] + (-1, 32))
    amax = np.abs(blocks).max(-1, keepdims=True)
    byte = np.maximum(np.where(amax > 0, np.frexp(amax)[1] - 1 + 127, 0) - down, 1)
    scale = np.exp2(byte - 127.0)
    codes = (blocks / scale).astype(np.float32).astype(dtype).astype(np.float64)
    return np.moveaxis((codes * scale).reshape(v.shape), -1, axis)


WIDE = False


def mx_kscale(k):
    if not WIDE:
        return np.ones(k)
    levels = np.array([10, -10, 5, -5, 0])
    a = np.random.permutation(np.resize(levels, k // 512 * 4)).reshape(k // 512, 4)
    idx = np.arange(k)
    return np.exp2(a[idx // 512, idx % 128 // 32])


BF16 = ml_dtypes.bfloat16


def bf(x):
    return np.asarray(x, np.float32).astype(BF16)


def f64(x):
    return np.asarray(x).astype(np.float64)


E2M1 = np.array([0.0, 0.5, 1.0, 1.5, 2.0, 3.0, 4.0, 6.0, -0.0, -0.5, -1.0, -1.5, -2.0, -3.0, -4.0, -6.0])


def pack_weight(w, fmt):
    k, n = w.shape
    w = f64(bf(w)).reshape(k // 32, 32, n)
    amax = np.abs(w).max(1)
    if fmt == "e4m3":
        byte = np.frexp(amax)[1] - 1 + 127 - 7
    else:
        mant, ex = np.frexp(amax / 6.0)
        byte = np.where(mant > 0.5, ex, ex - 1) + 127
    byte = np.clip(np.where(amax > 0, byte, 1), 1, 254)
    scaled = (w * np.exp2(127.0 - byte)[:, None, :]).reshape(k, n).astype(np.float32)
    by_word = np.ascontiguousarray(scaled.reshape(k // 512, 128, 4, n).transpose(0, 1, 3, 2))
    if fmt == "e4m3":
        words = by_word.astype(ml_dtypes.float8_e4m3fn).view(np.uint8)
    else:
        c = by_word.astype(ml_dtypes.float4_e2m1fn).view(np.uint8) & 0xF
        words = c[..., 0::2] | (c[..., 1::2] << 4)
    return np.ascontiguousarray(words), np.ascontiguousarray(byte.astype(np.uint8).reshape(k // 512, 16, n))


def unpack_weight(words, scales, fmt):
    g, p, n, _ = words.shape
    if fmt == "e4m3":
        vals = np.ascontiguousarray(words).view(ml_dtypes.float8_e4m3fn).astype(np.float64)
    else:
        nib = np.empty((g, p, n, 4), np.uint8)
        nib[..., 0::2] = words & 0xF
        nib[..., 1::2] = words >> 4
        vals = E2M1[nib]
    vals = vals * np.repeat(np.exp2(scales.astype(np.float64) - 127.0), 8, axis=1)[..., None]
    return vals.transpose(0, 1, 3, 2).reshape(g * 512, n)


B, N, D, HEAD, HALF = 4, 1024, 512, 512, 256
E = HEAD + HALF + HALF
EPS_RMS = 1e-6
EPS_NORM = 1e-12
FMT = "e4m3"


def setup_inputs():
    s = mx_kscale(D)
    x = bf(np.random.standard_normal((B, N, D)))
    g = bf((1.0 + 0.1 * np.random.standard_normal(D)) * s)
    words, scales = pack_weight(np.random.standard_normal((D, E)) / np.sqrt(D) / s[:, None], FMT)
    b1 = bf(np.random.standard_normal(E) * 0.3)
    return {"x": x,
            "g": g,
            "W1_words": words,
            "W1_scales": scales,
            "b1": b1}


def reference(x, g, W1_words, W1_scales, b1):
    x = f64(x)
    xn = x * (1.0 / np.sqrt(np.mean(np.square(x), axis=-1, keepdims=True) + EPS_RMS)) * f64(g)
    pre = (mxq(xn, 2, "e4m3") @ unpack_weight(W1_words, W1_scales, FMT)) + f64(b1)
    enriched = np.square(np.maximum(pre, 0.0))
    head = enriched[..., :HEAD]
    x_left = enriched[..., HEAD:HEAD + HALF]
    x_right = enriched[..., HEAD + HALF:]
    nrm = np.sqrt(np.sum(np.square(x_right), axis=-1, keepdims=True))
    xr_n = x_right / np.maximum(nrm, EPS_NORM)
    return head, x_left, xr_n

@@ -1,0 +1,214 @@
+from contextlib import ExitStack
+
+import concourse.mybir as mybir
+from concourse.masks import make_identity
+
+F32 = mybir.dt.float32
+BF16 = mybir.dt.bfloat16
+I32 = mybir.dt.int32
+U32 = mybir.dt.uint32
+U8 = mybir.dt.uint8
+FP8X4 = mybir.dt.float8_e4m3fn_x4
+ACT = mybir.ActivationFunctionType
+ALU = mybir.AluOpType
+
+P = 128
+PACK = 4
+TOKENS = 4 * 1024
+D = P * PACK
+HEAD = 512
+HALF = 256
+E = HEAD + 2 * HALF
+EPS_RMS = 1e-6
+EPS_NORM = 1e-12
+
+TILES = TOKENS // P
+CHUNK_TILES = 4
+CHUNK = CHUNK_TILES * P
+CHUNKS = TILES // CHUNK_TILES
+BLOCKS = E // P
+BANK_BLOCKS = 4
+HALVES = BLOCKS // BANK_BLOCKS
+
+FLOPS = 2 * TOKENS * D * E
+
+
+def tile_avey_pa_t_kernel(tc, x, g, W1_words, W1_scales, b1, out_0, out_1, out_2):
+    nc = tc.nc
+
+    x_rows = x.flatten_outer_dims().rearrange("(p n) k -> p n k", n=TILES)
+    head_rows = out_0.flatten_outer_dims().rearrange("(p n) f -> p n f", n=TILES)
+    left_rows = out_1.flatten_outer_dims().rearrange("(p n) f -> p n f", n=TILES)
+    right_rows = out_2.flatten_outer_dims().rearrange("(p n) f -> p n f", n=TILES)
+
+    with ExitStack() as stack:
+        const = stack.enter_context(tc.tile_pool(name="const", bufs=1))
+        x_pool = stack.enter_context(tc.tile_pool(name="x_pool", bufs=CHUNKS))
+        stat_pool = stack.enter_context(tc.tile_pool(name="stat_pool", bufs=3))
+        front_pool = stack.enter_context(tc.tile_pool(name="front_pool", bufs=2))
+        relu_pool = stack.enter_context(tc.tile_pool(name="relu_pool", bufs=3))
+        out_pool = stack.enter_context(tc.tile_pool(name="out_pool", bufs=3))
+        psum_front = stack.enter_context(tc.psum_pool(name="psum_front", bufs=2))
+        psum_acc = stack.enter_context(tc.psum_pool(name="psum_acc", bufs=3))
+        psum_back = stack.enter_context(tc.psum_pool(name="psum_back", bufs=3))
+
+        x_chunks = []
+        for c in range(CHUNKS):
+            x_chunk = x_pool.tile([P, CHUNK_TILES, D], BF16)
+            x_chunks.append(x_chunk)
+
+        def load_x(c):
+            tiles = slice(c * CHUNK_TILES, (c + 1) * CHUNK_TILES)
+            nc.sync.dma_start(out=x_chunks[c][:], in_=x_rows[:, tiles, :])
+
+        load_x(0)
+
+        w_codes = const.tile([P, E], U32, align_bytes=64)
+        nc.sync.dma_start(
+            out=w_codes[:].bitcast(I32),
+            in_=W1_words[0].rearrange("p n t -> p (n t)").bitcast(I32),
+        )
+        gain = const.tile([P, PACK], BF16)
+        nc.sync.dma_start(out=gain[:], in_=g.rearrange("(q t) -> q t", t=PACK))
+        b_rows = const.tile([BLOCKS, P], BF16)
+        nc.sync.dma_start(out=b_rows[:], in_=b1.rearrange("(b f) -> b f", f=P))
+        w_scales = const.tile([P, E], U8, align_bytes=64)
+        nc.vector.memset(w_scales[:].bitcast(I32), 0)
+        for quadrant in range(4):
+            nc.sync.dma_start(
+                out=w_scales[32 * quadrant : 32 * quadrant + 4, :].bitcast(I32),
+                in_=W1_scales[0, 4 * quadrant : 4 * quadrant + 4, :].bitcast(I32),
+            )
+        for c in range(1, CHUNKS):
+            load_x(c)
+
+        ident = const.tile([P, P], F32)
+        make_identity(nc, ident[:])
+        eps_rms = const.tile([P, 1], F32)
+        nc.vector.memset(eps_rms[:], EPS_RMS)
+        table_warm = const.tile([P, 1], F32)
+        nc.scalar.activation(out=table_warm[:], in_=eps_rms[:], func=ACT.Sqrt)
+
+        b_square = const.tile([P, P], F32)
+        nc.vector.memset(b_square[:], 0.0)
+        nc.vector.tensor_copy(out=b_square[0:BLOCKS, :], in_=b_rows[:])
+        b_turned = psum_front.tile([P, PACK, P], F32, tag="turned")
+        nc.tensor.transpose(out=b_turned[:, 0, :], in_=b_square[:], identity=ident[:])
+        bias = const.tile([P, BLOCKS], F32)
+        nc.vector.tensor_copy(out=bias[:], in_=b_turned[:, 0, 0:BLOCKS])
+
+        square_junk = const.tile([P, D], BF16)
+
+        def quantise_chunk(c):
+            x_chunk = x_chunks[c]
+            sumsq = stat_pool.tile([P, CHUNK_TILES], F32)
+            for j in range(CHUNK_TILES):
+                nc.scalar.activation(
+                    out=square_junk[:], in_=x_chunk[:, j, :], func=ACT.Square, accum_out=sumsq[:, j : j + 1]
+                )
+            rms = stat_pool.tile([P, CHUNK_TILES], F32)
+            nc.scalar.activation(out=rms[:], in_=sumsq[:], func=ACT.Sqrt, bias=eps_rms[:], scale=1.0 / D)
+            rstd = stat_pool.tile([P, CHUNK_TILES], F32)
+            nc.vector.reciprocal(out=rstd[:], in_=rms[:])
+
+            scaled = front_pool.tile([P, CHUNK_TILES, PACK, P], F32)
+            grouped = front_pool.tile([P, CHUNK_TILES, P, PACK], BF16, align_bytes=64)
+            for j in range(CHUNK_TILES):
+                nc.vector.tensor_scalar(
+                    out=scaled[:, j, :, :],
+                    in0=x_chunk[:, j, :].rearrange("p (q t) -> p t q", t=PACK),
+                    scalar1=rstd[:, j : j + 1],
+                    scalar2=None,
+                    op0=ALU.mult,
+                )
+            for j in range(CHUNK_TILES):
+                turned = psum_front.tile([P, PACK, P], F32, tag="turned")
+                for t in range(PACK):
+                    nc.tensor.transpose(out=turned[:, t, :], in_=scaled[:, j, t, :], identity=ident[:])
+                nc.vector.tensor_tensor(
+                    out=grouped[:, j, :, :],
+                    in0=turned[:].rearrange("q t r -> q r t"),
+                    in1=gain[:].unsqueeze(1).to_broadcast([P, P, PACK]),
+                    op=ALU.mult,
+                )
+            codes = front_pool.tile([P, CHUNK], U32, align_bytes=64)
+            scales = front_pool.tile([P, CHUNK], U8, align_bytes=64)
+            nc.vector.quantize_mx(
+                out=codes[:].bitcast(FP8X4),
+                scales=scales[:],
+                in_=grouped[:].rearrange("q j r t -> q (j r t)"),
+            )
+            return codes, scales
+
+        def project_chunk(c, codes, scales):
+            head_out = out_pool.tile([P, CHUNK_TILES, HEAD], F32)
+            pair_out = out_pool.tile([P, 2, CHUNK_TILES, HALF], F32)
+            for h in range(HALVES):
+                relu = relu_pool.tile([P, BANK_BLOCKS, CHUNK], F32)
+                for b in range(BANK_BLOCKS):
+                    block = h * BANK_BLOCKS + b
+                    features = slice(block * P, (block + 1) * P)
+                    acc = psum_acc.tile([P, CHUNK], F32)
+                    nc.tensor.matmul_mx(
+                        out=acc[:],
+                        lhsT=w_codes[:, features].bitcast(FP8X4),
+                        lhsT_scale=w_scales[:, features],
+                        rhs=codes[:].bitcast(FP8X4),
+                        rhs_scale=scales[:],
+                        start=True,
+                        stop=True,
+                    )
+                    nc.vector.tensor_scalar(
+                        out=relu[:, b, :],
+                        in0=acc[:],
+                        scalar1=bias[:, block : block + 1],
+                        scalar2=0.0,
+                        op0=ALU.add,
+                        op1=ALU.max,
+                    )
+                for j in range(CHUNK_TILES):
+                    back = psum_back.tile([P, BANK_BLOCKS, P], F32)
+                    for b in range(BANK_BLOCKS):
+                        nc.tensor.transpose(
+                            out=back[:, b, :], in_=relu[:, b, j * P : (j + 1) * P], identity=ident[:]
+                        )
+                    if h == 0:
+                        nc.scalar.activation(
+                            out=head_out[:, j, :], in_=back[:].rearrange("r b f -> r (b f)"), func=ACT.Square
+                        )
+                    else:
+                        nc.scalar.activation(
+                            out=pair_out[:, :, j, :],
+                            in_=back[:].rearrange("r (s b) f -> r s (b f)", s=2),
+                            func=ACT.Square,
+                        )
+
+            sumsq_right = stat_pool.tile([P, CHUNK_TILES], F32)
+            for j in range(CHUNK_TILES):
+                nc.scalar.activation(
+                    out=square_junk[:, 0:HALF],
+                    in_=pair_out[:, 1, j, :],
+                    func=ACT.Square,
+                    accum_out=sumsq_right[:, j : j + 1],
+                )
+            norm = stat_pool.tile([P, CHUNK_TILES], F32)
+            nc.scalar.activation(out=norm[:], in_=sumsq_right[:], func=ACT.Sqrt)
+            inv_norm = stat_pool.tile([P, CHUNK_TILES], F32)
+            nc.vector.tensor_scalar_max(out=norm[:], in0=norm[:], scalar1=EPS_NORM)
+            nc.vector.reciprocal(out=inv_norm[:], in_=norm[:])
+            for j in range(CHUNK_TILES):
+                nc.vector.tensor_scalar_mul(
+                    out=pair_out[:, 1, j, :], in0=pair_out[:, 1, j, :], scalar1=inv_norm[:, j : j + 1]
+                )
+
+            tiles = slice(c * CHUNK_TILES, (c + 1) * CHUNK_TILES)
+            nc.sync.dma_start(out=head_rows[:, tiles, :], in_=head_out[:])
+            nc.sync.dma_start(out=left_rows[:, tiles, :], in_=pair_out[:, 0, :, :])
+            nc.sync.dma_start(out=right_rows[:, tiles, :], in_=pair_out[:, 1, :, :])
+
+        quantised = quantise_chunk(0)
+        for c in range(CHUNKS):
+            codes, scales = quantised
+            if c + 1 < CHUNKS:
+                quantised = quantise_chunk(c + 1)
+            project_chunk(c, codes, scales)

@@ -27,8 +27,21 @@ CHUNK_TILES = 4
 CHUNK = CHUNK_TILES * P
 CHUNKS = TILES // CHUNK_TILES
 BLOCKS = E // P
-BANK_BLOCKS = 4
-HALVES = BLOCKS // BANK_BLOCKS
+RUN = 2
+WIDTH = RUN * P
+CHUNK_STEPS = BLOCKS // RUN
+STEPS = CHUNKS * CHUNK_STEPS
+BANK_TILES = 512 // WIDTH
+
+LEAD_SUMSQ = 12
+LEAD_SCALE = 8
+LEAD_TURN = 7
+LEAD_GAIN = 6
+LEAD_QUANTISE = 5
+LEAD_MULTIPLY = 1
+LAG_SQUARE = 1
+LAG_SUMSQ_RIGHT = 5
+LAG_NORMALISE = 9
 
 FLOPS = 2 * TOKENS * D * E
 
@@ -42,15 +55,17 @@ def tile_avey_pa_t_kernel(tc, x, g, W1_words, W1_scales, b1, out_0, out_1, out_2
     right_rows = out_2.flatten_outer_dims().rearrange("(p n) f -> p n f", n=TILES)
 
     with ExitStack() as stack:
+        stack.enter_context(tc.manual_schedule())
         const = stack.enter_context(tc.tile_pool(name="const", bufs=1))
         x_pool = stack.enter_context(tc.tile_pool(name="x_pool", bufs=CHUNKS))
-        stat_pool = stack.enter_context(tc.tile_pool(name="stat_pool", bufs=3))
-        front_pool = stack.enter_context(tc.tile_pool(name="front_pool", bufs=2))
+        stat_pool = stack.enter_context(tc.tile_pool(name="stat_pool", bufs=4))
+        tile_pool = stack.enter_context(tc.tile_pool(name="tile_pool", bufs=3))
+        code_pool = stack.enter_context(tc.tile_pool(name="code_pool", bufs=3))
         relu_pool = stack.enter_context(tc.tile_pool(name="relu_pool", bufs=3))
-        out_pool = stack.enter_context(tc.tile_pool(name="out_pool", bufs=3))
+        out_pool = stack.enter_context(tc.tile_pool(name="out_pool", bufs=4))
         psum_front = stack.enter_context(tc.psum_pool(name="psum_front", bufs=2))
-        psum_acc = stack.enter_context(tc.psum_pool(name="psum_acc", bufs=3))
-        psum_back = stack.enter_context(tc.psum_pool(name="psum_back", bufs=3))
+        psum_acc = stack.enter_context(tc.psum_pool(name="psum_acc", bufs=2 * RUN))
+        psum_back = stack.enter_context(tc.psum_pool(name="psum_back", bufs=2))
 
         x_chunks = []
         for c in range(CHUNKS):
@@ -99,116 +114,177 @@ def tile_avey_pa_t_kernel(tc, x, g, W1_words, W1_scales, b1, out_0, out_1, out_2
 
         square_junk = const.tile([P, D], BF16)
 
-        def quantise_chunk(c):
-            x_chunk = x_chunks[c]
-            sumsq = stat_pool.tile([P, CHUNK_TILES], F32)
-            for j in range(CHUNK_TILES):
-                nc.scalar.activation(
-                    out=square_junk[:], in_=x_chunk[:, j, :], func=ACT.Square, accum_out=sumsq[:, j : j + 1]
-                )
-            rms = stat_pool.tile([P, CHUNK_TILES], F32)
-            nc.scalar.activation(out=rms[:], in_=sumsq[:], func=ACT.Sqrt, bias=eps_rms[:], scale=1.0 / D)
-            rstd = stat_pool.tile([P, CHUNK_TILES], F32)
-            nc.vector.reciprocal(out=rstd[:], in_=rms[:])
+        sumsq, rms, rstd = {}, {}, {}
+        scaled, turned, grouped = {}, {}, {}
+        codes, scales = {}, {}
+        acc, relu = {}, {}
+        head_outs, quarters = {}, {}
+        sumsq_right, norm, inv_norm = {}, {}, {}
 
-            scaled = front_pool.tile([P, CHUNK_TILES, PACK, P], F32)
-            grouped = front_pool.tile([P, CHUNK_TILES, P, PACK], BF16, align_bytes=64)
-            for j in range(CHUNK_TILES):
-                nc.vector.tensor_scalar(
-                    out=scaled[:, j, :, :],
-                    in0=x_chunk[:, j, :].rearrange("p (q t) -> p t q", t=PACK),
-                    scalar1=rstd[:, j : j + 1],
-                    scalar2=None,
-                    op0=ALU.mult,
-                )
-            for j in range(CHUNK_TILES):
-                turned = psum_front.tile([P, PACK, P], F32, tag="turned")
-                for t in range(PACK):
-                    nc.tensor.transpose(out=turned[:, t, :], in_=scaled[:, j, t, :], identity=ident[:])
-                nc.vector.tensor_tensor(
-                    out=grouped[:, j, :, :],
-                    in0=turned[:].rearrange("q t r -> q r t"),
-                    in1=gain[:].unsqueeze(1).to_broadcast([P, P, PACK]),
-                    op=ALU.mult,
-                )
-            codes = front_pool.tile([P, CHUNK], U32, align_bytes=64)
-            scales = front_pool.tile([P, CHUNK], U8, align_bytes=64)
-            nc.vector.quantize_mx(
-                out=codes[:].bitcast(FP8X4),
-                scales=scales[:],
-                in_=grouped[:].rearrange("q j r t -> q (j r t)"),
+        def sum_squares(m):
+            c, j = divmod(m, CHUNK_TILES)
+            if j == 0:
+                sumsq_tile = stat_pool.tile([P, CHUNK_TILES], F32)
+                sumsq[c] = sumsq_tile
+            nc.scalar.activation(
+                out=square_junk[:], in_=x_chunks[c][:, j, :], func=ACT.Square, accum_out=sumsq[c][:, j : j + 1]
             )
-            return codes, scales
+            if j == CHUNK_TILES - 1:
+                rms_tile = stat_pool.tile([P, CHUNK_TILES], F32)
+                rms[c] = rms_tile
+                nc.scalar.activation(out=rms_tile[:], in_=sumsq[c][:], func=ACT.Sqrt, bias=eps_rms[:], scale=1.0 / D)
 
-        def project_chunk(c, codes, scales):
-            head_out = out_pool.tile([P, CHUNK_TILES, HEAD], F32)
-            pair_out = out_pool.tile([P, 2, CHUNK_TILES, HALF], F32)
-            for h in range(HALVES):
-                relu = relu_pool.tile([P, BANK_BLOCKS, CHUNK], F32)
-                for b in range(BANK_BLOCKS):
-                    block = h * BANK_BLOCKS + b
-                    features = slice(block * P, (block + 1) * P)
-                    acc = psum_acc.tile([P, CHUNK], F32)
-                    nc.tensor.matmul_mx(
-                        out=acc[:],
-                        lhsT=w_codes[:, features].bitcast(FP8X4),
-                        lhsT_scale=w_scales[:, features],
-                        rhs=codes[:].bitcast(FP8X4),
-                        rhs_scale=scales[:],
-                        start=True,
-                        stop=True,
-                    )
-                    nc.vector.tensor_scalar(
-                        out=relu[:, b, :],
-                        in0=acc[:],
-                        scalar1=bias[:, block : block + 1],
-                        scalar2=0.0,
-                        op0=ALU.add,
-                        op1=ALU.max,
-                    )
-                for j in range(CHUNK_TILES):
-                    back = psum_back.tile([P, BANK_BLOCKS, P], F32)
-                    for b in range(BANK_BLOCKS):
-                        nc.tensor.transpose(
-                            out=back[:, b, :], in_=relu[:, b, j * P : (j + 1) * P], identity=ident[:]
-                        )
-                    if h == 0:
-                        nc.scalar.activation(
-                            out=head_out[:, j, :], in_=back[:].rearrange("r b f -> r (b f)"), func=ACT.Square
-                        )
-                    else:
-                        nc.scalar.activation(
-                            out=pair_out[:, :, j, :],
-                            in_=back[:].rearrange("r (s b) f -> r s (b f)", s=2),
-                            func=ACT.Square,
-                        )
+        def invert_rms(m):
+            c, j = divmod(m, CHUNK_TILES)
+            if j == CHUNK_TILES - 1:
+                rstd_tile = stat_pool.tile([P, CHUNK_TILES], F32)
+                rstd[c] = rstd_tile
+                nc.vector.reciprocal(out=rstd_tile[:], in_=rms[c][:])
 
-            sumsq_right = stat_pool.tile([P, CHUNK_TILES], F32)
-            for j in range(CHUNK_TILES):
-                nc.scalar.activation(
-                    out=square_junk[:, 0:HALF],
-                    in_=pair_out[:, 1, j, :],
-                    func=ACT.Square,
-                    accum_out=sumsq_right[:, j : j + 1],
+        def scale_tile(m):
+            c, j = divmod(m, CHUNK_TILES)
+            scaled_tile = tile_pool.tile([P, PACK, P], F32)
+            scaled[m] = scaled_tile
+            nc.vector.tensor_scalar(
+                out=scaled_tile[:],
+                in0=x_chunks[c][:, j, :].rearrange("p (q t) -> p t q", t=PACK),
+                scalar1=rstd[c][:, j : j + 1],
+                scalar2=None,
+                op0=ALU.mult,
+            )
+
+        def turn_tile(m):
+            turned_tile = psum_front.tile([P, PACK, P], F32, tag="turned")
+            turned[m] = turned_tile
+            for t in range(PACK):
+                nc.tensor.transpose(out=turned_tile[:, t, :], in_=scaled[m][:, t, :], identity=ident[:])
+
+        def gain_tile(m):
+            grouped_tile = tile_pool.tile([P, P, PACK], BF16, align_bytes=64)
+            grouped[m] = grouped_tile
+            nc.vector.tensor_tensor(
+                out=grouped_tile[:],
+                in0=turned[m][:].rearrange("q t r -> q r t"),
+                in1=gain[:].unsqueeze(1).to_broadcast([P, P, PACK]),
+                op=ALU.mult,
+            )
+
+        def quantise_tile(m):
+            c, j = divmod(m, CHUNK_TILES)
+            if j == 0:
+                codes_tile = code_pool.tile([P, CHUNK], U32, align_bytes=64)
+                scales_tile = code_pool.tile([P, CHUNK], U8, align_bytes=64)
+                codes[c] = codes_tile
+                scales[c] = scales_tile
+            tokens = slice(j * P, (j + 1) * P)
+            nc.vector.quantize_mx(
+                out=codes[c][:, tokens].bitcast(FP8X4),
+                scales=scales[c][:, tokens],
+                in_=grouped[m][:].rearrange("q r t -> q (r t)"),
+            )
+
+        def multiply(s):
+            c, v = divmod(s, CHUNK_STEPS)
+            for b in range(RUN):
+                features = slice((v * RUN + b) * P, (v * RUN + b + 1) * P)
+                acc_tile = psum_acc.tile([P, CHUNK], F32)
+                acc[s, b] = acc_tile
+                nc.tensor.matmul_mx(
+                    out=acc_tile[:],
+                    lhsT=w_codes[:, features].bitcast(FP8X4),
+                    lhsT_scale=w_scales[:, features],
+                    rhs=codes[c][:].bitcast(FP8X4),
+                    rhs_scale=scales[c][:],
+                    start=True,
+                    stop=True,
                 )
-            norm = stat_pool.tile([P, CHUNK_TILES], F32)
-            nc.scalar.activation(out=norm[:], in_=sumsq_right[:], func=ACT.Sqrt)
-            inv_norm = stat_pool.tile([P, CHUNK_TILES], F32)
-            nc.vector.tensor_scalar_max(out=norm[:], in0=norm[:], scalar1=EPS_NORM)
-            nc.vector.reciprocal(out=inv_norm[:], in_=norm[:])
-            for j in range(CHUNK_TILES):
-                nc.vector.tensor_scalar_mul(
-                    out=pair_out[:, 1, j, :], in0=pair_out[:, 1, j, :], scalar1=inv_norm[:, j : j + 1]
+
+        def bias_relu(s):
+            v = s % CHUNK_STEPS
+            relu_tile = relu_pool.tile([P, RUN, CHUNK], F32)
+            relu[s] = relu_tile
+            for b in range(RUN):
+                block = v * RUN + b
+                nc.vector.tensor_scalar(
+                    out=relu_tile[:, b, :],
+                    in0=acc[s, b][:],
+                    scalar1=bias[:, block : block + 1],
+                    scalar2=0.0,
+                    op0=ALU.add,
+                    op1=ALU.max,
                 )
 
+        def turn_back_and_square(s):
+            c, v = divmod(s, CHUNK_STEPS)
             tiles = slice(c * CHUNK_TILES, (c + 1) * CHUNK_TILES)
-            nc.sync.dma_start(out=head_rows[:, tiles, :], in_=head_out[:])
-            nc.sync.dma_start(out=left_rows[:, tiles, :], in_=pair_out[:, 0, :, :])
-            nc.sync.dma_start(out=right_rows[:, tiles, :], in_=pair_out[:, 1, :, :])
+            if v == 0:
+                head_out = out_pool.tile([P, CHUNK_TILES, HEAD], F32)
+                pair_out = out_pool.tile([P, 2, CHUNK_TILES, HALF], F32)
+                head_outs[c] = head_out
+                quarters[c] = [head_out[:, :, 0:WIDTH], head_out[:, :, WIDTH:HEAD], pair_out[:, 0], pair_out[:, 1]]
+            quarter = quarters[c][v]
+            for first in range(0, CHUNK_TILES, BANK_TILES):
+                back = psum_back.tile([P, BANK_TILES, RUN, P], F32)
+                for i in range(BANK_TILES):
+                    tokens = slice((first + i) * P, (first + i + 1) * P)
+                    for b in range(RUN):
+                        nc.tensor.transpose(out=back[:, i, b, :], in_=relu[s][:, b, tokens], identity=ident[:])
+                nc.scalar.activation(
+                    out=quarter[:, first : first + BANK_TILES, :],
+                    in_=back[:].rearrange("r i b f -> r i (b f)"),
+                    func=ACT.Square,
+                )
+            if v == 1:
+                nc.sync.dma_start(out=head_rows[:, tiles, :], in_=head_outs[c][:])
+            if v == 2:
+                nc.sync.dma_start(out=left_rows[:, tiles, :], in_=quarter)
 
-        quantised = quantise_chunk(0)
-        for c in range(CHUNKS):
-            codes, scales = quantised
-            if c + 1 < CHUNKS:
-                quantised = quantise_chunk(c + 1)
-            project_chunk(c, codes, scales)
+        def sum_squares_right(m):
+            c, j = divmod(m, CHUNK_TILES)
+            if j == 0:
+                sumsq_right_tile = stat_pool.tile([P, CHUNK_TILES], F32)
+                sumsq_right[c] = sumsq_right_tile
+            nc.scalar.activation(
+                out=square_junk[:, 0:HALF],
+                in_=quarters[c][3][:, j, :],
+                func=ACT.Square,
+                accum_out=sumsq_right[c][:, j : j + 1],
+            )
+            if j == CHUNK_TILES - 1:
+                norm_tile = stat_pool.tile([P, CHUNK_TILES], F32)
+                norm[c] = norm_tile
+                nc.scalar.activation(out=norm_tile[:], in_=sumsq_right[c][:], func=ACT.Sqrt)
+
+        def invert_norm(m):
+            c, j = divmod(m, CHUNK_TILES)
+            if j == 0:
+                inv_norm_tile = stat_pool.tile([P, CHUNK_TILES], F32)
+                inv_norm[c] = inv_norm_tile
+                nc.vector.tensor_scalar_max(out=norm[c][:], in0=norm[c][:], scalar1=EPS_NORM)
+                nc.vector.reciprocal(out=inv_norm_tile[:], in_=norm[c][:])
+
+        def normalise_right(m):
+            c, j = divmod(m, CHUNK_TILES)
+            right = quarters[c][3]
+            nc.vector.tensor_scalar_mul(out=right[:, j, :], in0=right[:, j, :], scalar1=inv_norm[c][:, j : j + 1])
+            if j == CHUNK_TILES - 1:
+                tiles = slice(c * CHUNK_TILES, (c + 1) * CHUNK_TILES)
+                nc.sync.dma_start(out=right_rows[:, tiles, :], in_=right)
+
+        def run(stage, index, count):
+            if 0 <= index < count:
+                stage(index)
+
+        for k in range(-LEAD_SUMSQ, STEPS + LAG_NORMALISE):
+            run(sum_squares, k + LEAD_SUMSQ, TILES)
+            run(turn_back_and_square, k - LAG_SQUARE, STEPS)
+            run(turn_tile, k + LEAD_TURN, TILES)
+            run(multiply, k + LEAD_MULTIPLY, STEPS)
+            run(bias_relu, k, STEPS)
+            run(gain_tile, k + LEAD_GAIN, TILES)
+            run(quantise_tile, k + LEAD_QUANTISE, TILES)
+            run(invert_rms, k + LEAD_SUMSQ, TILES)
+            run(invert_norm, k - LAG_NORMALISE, TILES)
+            run(sum_squares_right, k - LAG_SUMSQ_RIGHT, TILES)
+            run(scale_tile, k + LEAD_SCALE, TILES)
+            run(normalise_right, k - LAG_NORMALISE, TILES)

@@ -145,12 +145,13 @@ def tile_avey_pa_t_kernel(tc, x, g, W1_words, W1_scales, b1, out_0, out_1, out_2
             c, j = divmod(m, CHUNK_TILES)
             scaled_tile = tile_pool.tile([P, PACK, P], F32)
             scaled[m] = scaled_tile
-            nc.vector.tensor_scalar(
+            nc.gpsimd.tensor_scalar(
                 out=scaled_tile[:],
                 in0=x_chunks[c][:, j, :].rearrange("p (q t) -> p t q", t=PACK),
                 scalar1=rstd[c][:, j : j + 1],
-                scalar2=None,
+                scalar2=0.0,
                 op0=ALU.mult,
+                op1=ALU.add,
             )
 
         def turn_tile(m):
@@ -266,7 +267,14 @@ def tile_avey_pa_t_kernel(tc, x, g, W1_words, W1_scales, b1, out_0, out_1, out_2
         def normalise_right(m):
             c, j = divmod(m, CHUNK_TILES)
             right = quarters[c][3]
-            nc.vector.tensor_scalar_mul(out=right[:, j, :], in0=right[:, j, :], scalar1=inv_norm[c][:, j : j + 1])
+            nc.gpsimd.tensor_scalar(
+                out=right[:, j, :],
+                in0=right[:, j, :],
+                scalar1=inv_norm[c][:, j : j + 1],
+                scalar2=0.0,
+                op0=ALU.mult,
+                op1=ALU.add,
+            )
             if j == CHUNK_TILES - 1:
                 tiles = slice(c * CHUNK_TILES, (c + 1) * CHUNK_TILES)
                 nc.sync.dma_start(out=right_rows[:, tiles, :], in_=right)

@@ -29,19 +29,19 @@ CHUNKS = TILES // CHUNK_TILES
 BLOCKS = E // P
 RUN = 2
 WIDTH = RUN * P
-CHUNK_STEPS = BLOCKS // RUN
-STEPS = CHUNKS * CHUNK_STEPS
+QUARTERS = E // WIDTH
+STEPS = CHUNKS * QUARTERS
 BANK_TILES = 512 // WIDTH
+RIGHT = QUARTERS - 1
 
-LEAD_SUMSQ = 12
+LEAD_SUMSQ = 14
+LEAD_INVERT = 12
 LEAD_SCALE = 8
 LEAD_TURN = 7
 LEAD_GAIN = 6
 LEAD_QUANTISE = 5
 LEAD_MULTIPLY = 1
-LAG_SQUARE = 1
-LAG_SUMSQ_RIGHT = 5
-LAG_NORMALISE = 9
+LEAD_SQUARE = -1
 
 FLOPS = 2 * TOKENS * D * E
 
@@ -53,6 +53,7 @@ def tile_avey_pa_t_kernel(tc, x, g, W1_words, W1_scales, b1, out_0, out_1, out_2
     head_rows = out_0.flatten_outer_dims().rearrange("(p n) f -> p n f", n=TILES)
     left_rows = out_1.flatten_outer_dims().rearrange("(p n) f -> p n f", n=TILES)
     right_rows = out_2.flatten_outer_dims().rearrange("(p n) f -> p n f", n=TILES)
+    quarter_rows = [head_rows[:, :, 0:WIDTH], head_rows[:, :, WIDTH:HEAD], left_rows, right_rows]
 
     with ExitStack() as stack:
         stack.enter_context(tc.manual_schedule())
@@ -62,21 +63,25 @@ def tile_avey_pa_t_kernel(tc, x, g, W1_words, W1_scales, b1, out_0, out_1, out_2
         tile_pool = stack.enter_context(tc.tile_pool(name="tile_pool", bufs=3))
         code_pool = stack.enter_context(tc.tile_pool(name="code_pool", bufs=3))
         relu_pool = stack.enter_context(tc.tile_pool(name="relu_pool", bufs=3))
-        out_pool = stack.enter_context(tc.tile_pool(name="out_pool", bufs=4))
+        out_pool = stack.enter_context(tc.tile_pool(name="out_pool", bufs=2 * QUARTERS))
         psum_front = stack.enter_context(tc.psum_pool(name="psum_front", bufs=2))
-        psum_acc = stack.enter_context(tc.psum_pool(name="psum_acc", bufs=2 * RUN))
-        psum_back = stack.enter_context(tc.psum_pool(name="psum_back", bufs=2))
+        psum_acc = stack.enter_context(tc.psum_pool(name="psum_acc", bufs=3))
+        psum_back = stack.enter_context(tc.psum_pool(name="psum_back", bufs=3))
 
         x_chunks = []
         for c in range(CHUNKS):
             x_chunk = x_pool.tile([P, CHUNK_TILES, D], BF16)
             x_chunks.append(x_chunk)
 
-        def load_x(c):
-            tiles = slice(c * CHUNK_TILES, (c + 1) * CHUNK_TILES)
-            nc.sync.dma_start(out=x_chunks[c][:], in_=x_rows[:, tiles, :])
+        def load_x(c, tiles_a_load):
+            for j in range(0, CHUNK_TILES, tiles_a_load):
+                first = c * CHUNK_TILES + j
+                nc.sync.dma_start(
+                    out=x_chunks[c][:, j : j + tiles_a_load, :], in_=x_rows[:, first : first + tiles_a_load, :]
+                )
 
-        load_x(0)
+        load_x(0, 1)
+        load_x(1, CHUNK_TILES)
 
         w_codes = const.tile([P, E], U32, align_bytes=64)
         nc.sync.dma_start(
@@ -94,8 +99,8 @@ def tile_avey_pa_t_kernel(tc, x, g, W1_words, W1_scales, b1, out_0, out_1, out_2
                 out=w_scales[32 * quadrant : 32 * quadrant + 4, :].bitcast(I32),
                 in_=W1_scales[0, 4 * quadrant : 4 * quadrant + 4, :].bitcast(I32),
             )
-        for c in range(1, CHUNKS):
-            load_x(c)
+        for c in range(2, CHUNKS):
+            load_x(c, CHUNK_TILES)
 
         ident = const.tile([P, P], F32)
         make_identity(nc, ident[:])
@@ -118,8 +123,7 @@ def tile_avey_pa_t_kernel(tc, x, g, W1_words, W1_scales, b1, out_0, out_1, out_2
         scaled, turned, grouped = {}, {}, {}
         codes, scales = {}, {}
         acc, relu = {}, {}
-        head_outs, quarters = {}, {}
-        sumsq_right, norm, inv_norm = {}, {}, {}
+        right, sumsq_right, norm, inv_norm = {}, {}, {}, {}
 
         def sum_squares(m):
             c, j = divmod(m, CHUNK_TILES)
@@ -184,10 +188,14 @@ def tile_avey_pa_t_kernel(tc, x, g, W1_words, W1_scales, b1, out_0, out_1, out_2
                 in_=grouped[m][:].rearrange("q r t -> q (r t)"),
             )
 
+        def quarter_of(v):
+            return (v + RIGHT) % QUARTERS
+
         def multiply(s):
-            c, v = divmod(s, CHUNK_STEPS)
+            c, v = divmod(s, QUARTERS)
             for b in range(RUN):
-                features = slice((v * RUN + b) * P, (v * RUN + b + 1) * P)
+                block = quarter_of(v) * RUN + b
+                features = slice(block * P, (block + 1) * P)
                 acc_tile = psum_acc.tile([P, CHUNK], F32)
                 acc[s, b] = acc_tile
                 nc.tensor.matmul_mx(
@@ -201,11 +209,11 @@ def tile_avey_pa_t_kernel(tc, x, g, W1_words, W1_scales, b1, out_0, out_1, out_2
                 )
 
         def bias_relu(s):
-            v = s % CHUNK_STEPS
+            v = s % QUARTERS
             relu_tile = relu_pool.tile([P, RUN, CHUNK], F32)
             relu[s] = relu_tile
             for b in range(RUN):
-                block = v * RUN + b
+                block = quarter_of(v) * RUN + b
                 nc.vector.tensor_scalar(
                     out=relu_tile[:, b, :],
                     in0=acc[s, b][:],
@@ -215,15 +223,13 @@ def tile_avey_pa_t_kernel(tc, x, g, W1_words, W1_scales, b1, out_0, out_1, out_2
                     op1=ALU.max,
                 )
 
-        def turn_back_and_square(s):
-            c, v = divmod(s, CHUNK_STEPS)
+        def store_quarter(c, quarter, tile):
             tiles = slice(c * CHUNK_TILES, (c + 1) * CHUNK_TILES)
-            if v == 0:
-                head_out = out_pool.tile([P, CHUNK_TILES, HEAD], F32)
-                pair_out = out_pool.tile([P, 2, CHUNK_TILES, HALF], F32)
-                head_outs[c] = head_out
-                quarters[c] = [head_out[:, :, 0:WIDTH], head_out[:, :, WIDTH:HEAD], pair_out[:, 0], pair_out[:, 1]]
-            quarter = quarters[c][v]
+            nc.sync.dma_start(out=quarter_rows[quarter][:, tiles, :], in_=tile[:])
+
+        def turn_back_and_square(s):
+            c, v = divmod(s, QUARTERS)
+            squared = out_pool.tile([P, CHUNK_TILES, WIDTH], F32)
             for first in range(0, CHUNK_TILES, BANK_TILES):
                 back = psum_back.tile([P, BANK_TILES, RUN, P], F32)
                 for i in range(BANK_TILES):
@@ -231,68 +237,70 @@ def tile_avey_pa_t_kernel(tc, x, g, W1_words, W1_scales, b1, out_0, out_1, out_2
                     for b in range(RUN):
                         nc.tensor.transpose(out=back[:, i, b, :], in_=relu[s][:, b, tokens], identity=ident[:])
                 nc.scalar.activation(
-                    out=quarter[:, first : first + BANK_TILES, :],
+                    out=squared[:, first : first + BANK_TILES, :],
                     in_=back[:].rearrange("r i b f -> r i (b f)"),
                     func=ACT.Square,
                 )
-            if v == 1:
-                nc.sync.dma_start(out=head_rows[:, tiles, :], in_=head_outs[c][:])
-            if v == 2:
-                nc.sync.dma_start(out=left_rows[:, tiles, :], in_=quarter)
+            if quarter_of(v) == RIGHT:
+                right[c] = squared
+            else:
+                store_quarter(c, quarter_of(v), squared)
 
-        def sum_squares_right(m):
-            c, j = divmod(m, CHUNK_TILES)
-            if j == 0:
+        def sum_squares_right(s):
+            c, v = divmod(s, QUARTERS)
+            if v == 0:
                 sumsq_right_tile = stat_pool.tile([P, CHUNK_TILES], F32)
                 sumsq_right[c] = sumsq_right_tile
-            nc.scalar.activation(
-                out=square_junk[:, 0:HALF],
-                in_=quarters[c][3][:, j, :],
-                func=ACT.Square,
-                accum_out=sumsq_right[c][:, j : j + 1],
-            )
-            if j == CHUNK_TILES - 1:
+            if v < 2:
+                for j in range(2 * v, 2 * v + 2):
+                    nc.scalar.activation(
+                        out=square_junk[:, 0:WIDTH],
+                        in_=right[c][:, j, :],
+                        func=ACT.Square,
+                        accum_out=sumsq_right[c][:, j : j + 1],
+                    )
+            if v == 1:
                 norm_tile = stat_pool.tile([P, CHUNK_TILES], F32)
                 norm[c] = norm_tile
                 nc.scalar.activation(out=norm_tile[:], in_=sumsq_right[c][:], func=ACT.Sqrt)
 
-        def invert_norm(m):
-            c, j = divmod(m, CHUNK_TILES)
-            if j == 0:
+        def invert_norm(s):
+            c, v = divmod(s, QUARTERS)
+            if v == 2:
                 inv_norm_tile = stat_pool.tile([P, CHUNK_TILES], F32)
                 inv_norm[c] = inv_norm_tile
                 nc.vector.tensor_scalar_max(out=norm[c][:], in0=norm[c][:], scalar1=EPS_NORM)
                 nc.vector.reciprocal(out=inv_norm_tile[:], in_=norm[c][:])
 
-        def normalise_right(m):
-            c, j = divmod(m, CHUNK_TILES)
-            right = quarters[c][3]
-            nc.gpsimd.tensor_scalar(
-                out=right[:, j, :],
-                in0=right[:, j, :],
-                scalar1=inv_norm[c][:, j : j + 1],
-                scalar2=0.0,
-                op0=ALU.mult,
-                op1=ALU.add,
-            )
-            if j == CHUNK_TILES - 1:
-                tiles = slice(c * CHUNK_TILES, (c + 1) * CHUNK_TILES)
-                nc.sync.dma_start(out=right_rows[:, tiles, :], in_=right)
+        def normalise_right(s):
+            c, v = divmod(s, QUARTERS)
+            if v >= 2:
+                for j in range(2 * (v - 2), 2 * (v - 2) + 2):
+                    nc.gpsimd.tensor_scalar(
+                        out=right[c][:, j, :],
+                        in0=right[c][:, j, :],
+                        scalar1=inv_norm[c][:, j : j + 1],
+                        scalar2=0.0,
+                        op0=ALU.mult,
+                        op1=ALU.add,
+                    )
+            if v == 3:
+                store_quarter(c, RIGHT, right[c])
 
         def run(stage, index, count):
             if 0 <= index < count:
                 stage(index)
 
-        for k in range(-LEAD_SUMSQ, STEPS + LAG_NORMALISE):
+        for k in range(-LEAD_SUMSQ, STEPS - LEAD_SQUARE):
             run(sum_squares, k + LEAD_SUMSQ, TILES)
-            run(turn_back_and_square, k - LAG_SQUARE, STEPS)
+            run(bias_relu, k, STEPS)
+            run(turn_back_and_square, k + LEAD_SQUARE, STEPS)
             run(turn_tile, k + LEAD_TURN, TILES)
             run(multiply, k + LEAD_MULTIPLY, STEPS)
-            run(bias_relu, k, STEPS)
             run(gain_tile, k + LEAD_GAIN, TILES)
             run(quantise_tile, k + LEAD_QUANTISE, TILES)
-            run(invert_rms, k + LEAD_SUMSQ, TILES)
-            run(invert_norm, k - LAG_NORMALISE, TILES)
-            run(sum_squares_right, k - LAG_SUMSQ_RIGHT, TILES)
+            run(invert_rms, k + LEAD_INVERT, TILES)
+            run(invert_norm, k + LEAD_SQUARE, STEPS)
+            run(sum_squares_right, k + LEAD_SQUARE, STEPS)
             run(scale_tile, k + LEAD_SCALE, TILES)
-            run(normalise_right, k - LAG_NORMALISE, TILES)
+            run(normalise_right, k + LEAD_SQUARE, STEPS)

@@ -34,14 +34,14 @@ STEPS = CHUNKS * QUARTERS
 BANK_TILES = 512 // WIDTH
 RIGHT = QUARTERS - 1
 
-LEAD_SUMSQ = 14
-LEAD_INVERT = 12
+LEAD_SUMSQ = 18
 LEAD_SCALE = 8
 LEAD_TURN = 7
 LEAD_GAIN = 6
 LEAD_QUANTISE = 5
 LEAD_MULTIPLY = 1
 LEAD_SQUARE = -1
+ASSISTED_TILES = 2 * CHUNK_TILES
 
 FLOPS = 2 * TOKENS * D * E
 
@@ -80,6 +80,8 @@ def tile_avey_pa_t_kernel(tc, x, g, W1_words, W1_scales, b1, out_0, out_1, out_2
                     out=x_chunks[c][:, j : j + tiles_a_load, :], in_=x_rows[:, first : first + tiles_a_load, :]
                 )
 
+        b_rows = const.tile([BLOCKS, P], BF16)
+        nc.sync.dma_start(out=b_rows[:], in_=b1.rearrange("(b f) -> b f", f=P))
         load_x(0, 1)
         load_x(1, CHUNK_TILES)
 
@@ -90,8 +92,6 @@ def tile_avey_pa_t_kernel(tc, x, g, W1_words, W1_scales, b1, out_0, out_1, out_2
         )
         gain = const.tile([P, PACK], BF16)
         nc.sync.dma_start(out=gain[:], in_=g.rearrange("(q t) -> q t", t=PACK))
-        b_rows = const.tile([BLOCKS, P], BF16)
-        nc.sync.dma_start(out=b_rows[:], in_=b1.rearrange("(b f) -> b f", f=P))
         w_scales = const.tile([P, E], U8, align_bytes=64)
         nc.vector.memset(w_scales[:].bitcast(I32), 0)
         for quadrant in range(4):
@@ -107,7 +107,7 @@ def tile_avey_pa_t_kernel(tc, x, g, W1_words, W1_scales, b1, out_0, out_1, out_2
         eps_rms = const.tile([P, 1], F32)
         nc.vector.memset(eps_rms[:], EPS_RMS)
         table_warm = const.tile([P, 1], F32)
-        nc.scalar.activation(out=table_warm[:], in_=eps_rms[:], func=ACT.Sqrt)
+        nc.scalar.activation(out=table_warm[:], in_=eps_rms[:], func=ACT.Abs_reciprocal_sqrt)
 
         b_square = const.tile([P, P], F32)
         nc.vector.memset(b_square[:], 0.0)
@@ -118,6 +118,7 @@ def tile_avey_pa_t_kernel(tc, x, g, W1_words, W1_scales, b1, out_0, out_1, out_2
         nc.vector.tensor_copy(out=bias[:], in_=b_turned[:, 0, 0:BLOCKS])
 
         square_junk = const.tile([P, D], BF16)
+        assist_junk = const.tile([P, D], F32)
 
         sumsq, rms, rstd = {}, {}, {}
         scaled, turned, grouped = {}, {}, {}
@@ -130,20 +131,26 @@ def tile_avey_pa_t_kernel(tc, x, g, W1_words, W1_scales, b1, out_0, out_1, out_2
             if j == 0:
                 sumsq_tile = stat_pool.tile([P, CHUNK_TILES], F32)
                 sumsq[c] = sumsq_tile
-            nc.scalar.activation(
-                out=square_junk[:], in_=x_chunks[c][:, j, :], func=ACT.Square, accum_out=sumsq[c][:, j : j + 1]
-            )
-            if j == CHUNK_TILES - 1:
-                rms_tile = stat_pool.tile([P, CHUNK_TILES], F32)
-                rms[c] = rms_tile
-                nc.scalar.activation(out=rms_tile[:], in_=sumsq[c][:], func=ACT.Sqrt, bias=eps_rms[:], scale=1.0 / D)
-
-        def invert_rms(m):
-            c, j = divmod(m, CHUNK_TILES)
+            if m < ASSISTED_TILES and m % 2 == 1:
+                nc.vector.scalar_tensor_tensor(
+                    out=assist_junk[:],
+                    in0=x_chunks[c][:, j, :],
+                    scalar=1.0,
+                    in1=x_chunks[c][:, j, :],
+                    op0=ALU.mult,
+                    op1=ALU.mult,
+                    accum_out=sumsq[c][:, j : j + 1],
+                )
+            else:
+                nc.scalar.activation(
+                    out=square_junk[:], in_=x_chunks[c][:, j, :], func=ACT.Square, accum_out=sumsq[c][:, j : j + 1]
+                )
             if j == CHUNK_TILES - 1:
                 rstd_tile = stat_pool.tile([P, CHUNK_TILES], F32)
                 rstd[c] = rstd_tile
-                nc.vector.reciprocal(out=rstd_tile[:], in_=rms[c][:])
+                nc.scalar.activation(
+                    out=rstd_tile[:], in_=sumsq[c][:], func=ACT.Abs_reciprocal_sqrt, bias=eps_rms[:], scale=1.0 / D
+                )
 
         def scale_tile(m):
             c, j = divmod(m, CHUNK_TILES)
@@ -165,10 +172,12 @@ def tile_avey_pa_t_kernel(tc, x, g, W1_words, W1_scales, b1, out_0, out_1, out_2
                 nc.tensor.transpose(out=turned_tile[:, t, :], in_=scaled[m][:, t, :], identity=ident[:])
 
         def gain_tile(m):
-            grouped_tile = tile_pool.tile([P, P, PACK], BF16, align_bytes=64)
-            grouped[m] = grouped_tile
+            c, j = divmod(m, CHUNK_TILES)
+            if j == 0:
+                grouped_tile = tile_pool.tile([P, CHUNK_TILES, P, PACK], BF16, align_bytes=64)
+                grouped[c] = grouped_tile
             nc.vector.tensor_tensor(
-                out=grouped_tile[:],
+                out=grouped[c][:, j, :, :],
                 in0=turned[m][:].rearrange("q t r -> q r t"),
                 in1=gain[:].unsqueeze(1).to_broadcast([P, P, PACK]),
                 op=ALU.mult,
@@ -176,17 +185,16 @@ def tile_avey_pa_t_kernel(tc, x, g, W1_words, W1_scales, b1, out_0, out_1, out_2
 
         def quantise_tile(m):
             c, j = divmod(m, CHUNK_TILES)
-            if j == 0:
+            if j == CHUNK_TILES - 1:
                 codes_tile = code_pool.tile([P, CHUNK], U32, align_bytes=64)
                 scales_tile = code_pool.tile([P, CHUNK], U8, align_bytes=64)
                 codes[c] = codes_tile
                 scales[c] = scales_tile
-            tokens = slice(j * P, (j + 1) * P)
-            nc.vector.quantize_mx(
-                out=codes[c][:, tokens].bitcast(FP8X4),
-                scales=scales[c][:, tokens],
-                in_=grouped[m][:].rearrange("q r t -> q (r t)"),
-            )
+                nc.vector.quantize_mx(
+                    out=codes_tile[:].bitcast(FP8X4),
+                    scales=scales_tile[:],
+                    in_=grouped[c][:].rearrange("q j r t -> q (j r t)"),
+                )
 
         def quarter_of(v):
             return (v + RIGHT) % QUARTERS
@@ -262,15 +270,14 @@ def tile_avey_pa_t_kernel(tc, x, g, W1_words, W1_scales, b1, out_0, out_1, out_2
             if v == 1:
                 norm_tile = stat_pool.tile([P, CHUNK_TILES], F32)
                 norm[c] = norm_tile
-                nc.scalar.activation(out=norm_tile[:], in_=sumsq_right[c][:], func=ACT.Sqrt)
+                nc.scalar.activation(out=norm_tile[:], in_=sumsq_right[c][:], func=ACT.Abs_reciprocal_sqrt)
 
         def invert_norm(s):
             c, v = divmod(s, QUARTERS)
             if v == 2:
                 inv_norm_tile = stat_pool.tile([P, CHUNK_TILES], F32)
                 inv_norm[c] = inv_norm_tile
-                nc.vector.tensor_scalar_max(out=norm[c][:], in0=norm[c][:], scalar1=EPS_NORM)
-                nc.vector.reciprocal(out=inv_norm_tile[:], in_=norm[c][:])
+                nc.vector.tensor_scalar_min(out=inv_norm_tile[:], in0=norm[c][:], scalar1=1.0 / EPS_NORM)
 
         def normalise_right(s):
             c, v = divmod(s, QUARTERS)
@@ -299,7 +306,6 @@ def tile_avey_pa_t_kernel(tc, x, g, W1_words, W1_scales, b1, out_0, out_1, out_2
             run(multiply, k + LEAD_MULTIPLY, STEPS)
             run(gain_tile, k + LEAD_GAIN, TILES)
             run(quantise_tile, k + LEAD_QUANTISE, TILES)
-            run(invert_rms, k + LEAD_INVERT, TILES)
             run(invert_norm, k + LEAD_SQUARE, STEPS)
             run(sum_squares_right, k + LEAD_SQUARE, STEPS)
             run(scale_tile, k + LEAD_SCALE, TILES)

@@ -145,12 +145,25 @@ def tile_avey_pa_t_kernel(tc, x, g, W1_words, W1_scales, b1, out_0, out_1, out_2
                 nc.scalar.activation(
                     out=square_junk[:], in_=x_chunks[c][:, j, :], func=ACT.Square, accum_out=sumsq[c][:, j : j + 1]
                 )
-            if j == CHUNK_TILES - 1:
+
+        def root_rms(m):
+            c, j = divmod(m, CHUNK_TILES)
+            if j == 0:
                 rstd_tile = stat_pool.tile([P, CHUNK_TILES], F32)
                 rstd[c] = rstd_tile
-                nc.scalar.activation(
-                    out=rstd_tile[:], in_=sumsq[c][:], func=ACT.Abs_reciprocal_sqrt, bias=eps_rms[:], scale=1.0 / D
-                )
+            if c == 0:
+                tiles = slice(j, j + 1)
+            elif j == CHUNK_TILES - 1:
+                tiles = slice(0, CHUNK_TILES)
+            else:
+                return
+            nc.scalar.activation(
+                out=rstd[c][:, tiles],
+                in_=sumsq[c][:, tiles],
+                func=ACT.Abs_reciprocal_sqrt,
+                bias=eps_rms[:],
+                scale=1.0 / D,
+            )
 
         def scale_tile(m):
             c, j = divmod(m, CHUNK_TILES)
@@ -216,24 +229,24 @@ def tile_avey_pa_t_kernel(tc, x, g, W1_words, W1_scales, b1, out_0, out_1, out_2
                     stop=True,
                 )
 
-        def bias_relu(s):
+        def bias_relu(s, b):
             v = s % QUARTERS
-            relu_tile = relu_pool.tile([P, RUN, CHUNK], F32)
-            relu[s] = relu_tile
-            for b in range(RUN):
-                block = quarter_of(v) * RUN + b
-                nc.vector.tensor_scalar(
-                    out=relu_tile[:, b, :],
-                    in0=acc[s, b][:],
-                    scalar1=bias[:, block : block + 1],
-                    scalar2=0.0,
-                    op0=ALU.add,
-                    op1=ALU.max,
-                )
+            if b == 0:
+                relu_tile = relu_pool.tile([P, RUN, CHUNK], F32)
+                relu[s] = relu_tile
+            block = quarter_of(v) * RUN + b
+            nc.vector.tensor_scalar(
+                out=relu[s][:, b, :],
+                in0=acc[s, b][:],
+                scalar1=bias[:, block : block + 1],
+                scalar2=0.0,
+                op0=ALU.add,
+                op1=ALU.max,
+            )
 
-        def store_quarter(c, quarter, tile):
-            tiles = slice(c * CHUNK_TILES, (c + 1) * CHUNK_TILES)
-            nc.sync.dma_start(out=quarter_rows[quarter][:, tiles, :], in_=tile[:])
+        def store_pair(c, quarter, tile, first):
+            rows = slice(c * CHUNK_TILES + first, c * CHUNK_TILES + first + BANK_TILES)
+            nc.sync.dma_start(out=quarter_rows[quarter][:, rows, :], in_=tile[:, first : first + BANK_TILES, :])
 
         def turn_back_and_square(s):
             c, v = divmod(s, QUARTERS)
@@ -249,10 +262,10 @@ def tile_avey_pa_t_kernel(tc, x, g, W1_words, W1_scales, b1, out_0, out_1, out_2
                     in_=back[:].rearrange("r i b f -> r i (b f)"),
                     func=ACT.Square,
                 )
+                if quarter_of(v) != RIGHT:
+                    store_pair(c, quarter_of(v), squared, first)
             if quarter_of(v) == RIGHT:
                 right[c] = squared
-            else:
-                store_quarter(c, quarter_of(v), squared)
 
         def sum_squares_right(s):
             c, v = divmod(s, QUARTERS)
@@ -291,8 +304,7 @@ def tile_avey_pa_t_kernel(tc, x, g, W1_words, W1_scales, b1, out_0, out_1, out_2
                         op0=ALU.mult,
                         op1=ALU.add,
                     )
-            if v == 3:
-                store_quarter(c, RIGHT, right[c])
+                store_pair(c, RIGHT, right[c], 2 * (v - 2))
 
         def run(stage, index, count):
             if 0 <= index < count:
@@ -300,7 +312,9 @@ def tile_avey_pa_t_kernel(tc, x, g, W1_words, W1_scales, b1, out_0, out_1, out_2
 
         for k in range(-LEAD_SUMSQ, STEPS - LEAD_SQUARE):
             run(sum_squares, k + LEAD_SUMSQ, TILES)
-            run(bias_relu, k, STEPS)
+            run(root_rms, k + LEAD_SUMSQ - 1, TILES)
+            run(lambda s: bias_relu(s, 0), k, STEPS)
+            run(lambda s: bias_relu(s, 1), k, STEPS)
             run(turn_back_and_square, k + LEAD_SQUARE, STEPS)
             run(turn_tile, k + LEAD_TURN, TILES)
             run(multiply, k + LEAD_MULTIPLY, STEPS)

@@ -106,6 +106,10 @@ def tile_avey_pa_t_kernel(tc, x, g, W1_words, W1_scales, b1, out_0, out_1, out_2
         make_identity(nc, ident[:])
         eps_rms = const.tile([P, 1], F32)
         nc.vector.memset(eps_rms[:], EPS_RMS)
+        plus_floor = const.tile([P, 1], F32)
+        nc.vector.memset(plus_floor[:], EPS_NORM * EPS_NORM)
+        minus_floor = const.tile([P, 1], F32)
+        nc.vector.memset(minus_floor[:], -EPS_NORM * EPS_NORM)
         table_warm = const.tile([P, 1], F32)
         nc.scalar.activation(out=table_warm[:], in_=eps_rms[:], func=ACT.Abs_reciprocal_sqrt)
 
@@ -264,6 +268,8 @@ def tile_avey_pa_t_kernel(tc, x, g, W1_words, W1_scales, b1, out_0, out_1, out_2
                 )
                 if quarter_of(v) != RIGHT:
                     store_pair(c, quarter_of(v), squared, first)
+                if first == 0:
+                    invert_norm(s)
             if quarter_of(v) == RIGHT:
                 right[c] = squared
 
@@ -280,17 +286,22 @@ def tile_avey_pa_t_kernel(tc, x, g, W1_words, W1_scales, b1, out_0, out_1, out_2
                         func=ACT.Square,
                         accum_out=sumsq_right[c][:, j : j + 1],
                     )
-            if v == 1:
+
+        def clamp_norm(s):
+            c, v = divmod(s, QUARTERS)
+            if v == 2:
                 norm_tile = stat_pool.tile([P, CHUNK_TILES], F32)
                 norm[c] = norm_tile
-                nc.scalar.activation(out=norm_tile[:], in_=sumsq_right[c][:], func=ACT.Abs_reciprocal_sqrt)
+                nc.scalar.activation(out=norm_tile[:], in_=sumsq_right[c][:], func=ACT.Relu, bias=minus_floor[:])
 
         def invert_norm(s):
             c, v = divmod(s, QUARTERS)
             if v == 2:
                 inv_norm_tile = stat_pool.tile([P, CHUNK_TILES], F32)
                 inv_norm[c] = inv_norm_tile
-                nc.vector.tensor_scalar_min(out=inv_norm_tile[:], in0=norm[c][:], scalar1=1.0 / EPS_NORM)
+                nc.scalar.activation(
+                    out=inv_norm_tile[:], in_=norm[c][:], func=ACT.Abs_reciprocal_sqrt, bias=plus_floor[:]
+                )
 
         def normalise_right(s):
             c, v = divmod(s, QUARTERS)
@@ -313,6 +324,7 @@ def tile_avey_pa_t_kernel(tc, x, g, W1_words, W1_scales, b1, out_0, out_1, out_2
         for k in range(-LEAD_SUMSQ, STEPS - LEAD_SQUARE):
             run(sum_squares, k + LEAD_SUMSQ, TILES)
             run(root_rms, k + LEAD_SUMSQ - 1, TILES)
+            run(clamp_norm, k + LEAD_SQUARE, STEPS)
             run(lambda s: bias_relu(s, 0), k, STEPS)
             run(lambda s: bias_relu(s, 1), k, STEPS)
             run(turn_back_and_square, k + LEAD_SQUARE, STEPS)
@@ -320,7 +332,6 @@ def tile_avey_pa_t_kernel(tc, x, g, W1_words, W1_scales, b1, out_0, out_1, out_2
             run(multiply, k + LEAD_MULTIPLY, STEPS)
             run(gain_tile, k + LEAD_GAIN, TILES)
             run(quantise_tile, k + LEAD_QUANTISE, TILES)
-            run(invert_norm, k + LEAD_SQUARE, STEPS)
             run(sum_squares_right, k + LEAD_SQUARE, STEPS)
             run(scale_tile, k + LEAD_SCALE, TILES)
             run(normalise_right, k + LEAD_SQUARE, STEPS)

@@ -328,8 +328,8 @@ def tile_avey_pa_t_kernel(tc, x, g, W1_words, W1_scales, b1, out_0, out_1, out_2
             run(lambda s: bias_relu(s, 0), k, STEPS)
             run(lambda s: bias_relu(s, 1), k, STEPS)
             run(turn_back_and_square, k + LEAD_SQUARE, STEPS)
-            run(turn_tile, k + LEAD_TURN, TILES)
             run(multiply, k + LEAD_MULTIPLY, STEPS)
+            run(turn_tile, k + LEAD_TURN, TILES)
             run(gain_tile, k + LEAD_GAIN, TILES)
             run(quantise_tile, k + LEAD_QUANTISE, TILES)
             run(sum_squares_right, k + LEAD_SQUARE, STEPS)

from contextlib import ExitStack

import concourse.mybir as mybir
from concourse.masks import make_identity

F32 = mybir.dt.float32
BF16 = mybir.dt.bfloat16
I32 = mybir.dt.int32
U32 = mybir.dt.uint32
U8 = mybir.dt.uint8
FP8X4 = mybir.dt.float8_e4m3fn_x4
ACT = mybir.ActivationFunctionType
ALU = mybir.AluOpType

P = 128
PACK = 4
TOKENS = 4 * 1024
D = P * PACK
HEAD = 512
HALF = 256
E = HEAD + 2 * HALF
EPS_RMS = 1e-6
EPS_NORM = 1e-12

TILES = TOKENS // P
CHUNK_TILES = 4
CHUNK = CHUNK_TILES * P
CHUNKS = TILES // CHUNK_TILES
BLOCKS = E // P
RUN = 2
WIDTH = RUN * P
QUARTERS = E // WIDTH
STEPS = CHUNKS * QUARTERS
BANK_TILES = 512 // WIDTH
RIGHT = QUARTERS - 1

LEAD_SUMSQ = 18
LEAD_SCALE = 8
LEAD_TURN = 7
LEAD_GAIN = 6
LEAD_QUANTISE = 5
LEAD_MULTIPLY = 1
LEAD_SQUARE = -1
ASSISTED_TILES = 2 * CHUNK_TILES

FLOPS = 2 * TOKENS * D * E


def tile_avey_pa_t_kernel(tc, x, g, W1_words, W1_scales, b1, out_0, out_1, out_2):
    nc = tc.nc

    x_rows = x.flatten_outer_dims().rearrange("(p n) k -> p n k", n=TILES)
    head_rows = out_0.flatten_outer_dims().rearrange("(p n) f -> p n f", n=TILES)
    left_rows = out_1.flatten_outer_dims().rearrange("(p n) f -> p n f", n=TILES)
    right_rows = out_2.flatten_outer_dims().rearrange("(p n) f -> p n f", n=TILES)
    quarter_rows = [head_rows[:, :, 0:WIDTH], head_rows[:, :, WIDTH:HEAD], left_rows, right_rows]

    with ExitStack() as stack:
        stack.enter_context(tc.manual_schedule())
        const = stack.enter_context(tc.tile_pool(name="const", bufs=1))
        x_pool = stack.enter_context(tc.tile_pool(name="x_pool", bufs=CHUNKS))
        stat_pool = stack.enter_context(tc.tile_pool(name="stat_pool", bufs=4))
        tile_pool = stack.enter_context(tc.tile_pool(name="tile_pool", bufs=3))
        code_pool = stack.enter_context(tc.tile_pool(name="code_pool", bufs=3))
        relu_pool = stack.enter_context(tc.tile_pool(name="relu_pool", bufs=3))
        out_pool = stack.enter_context(tc.tile_pool(name="out_pool", bufs=2 * QUARTERS))
        psum_front = stack.enter_context(tc.psum_pool(name="psum_front", bufs=2))
        psum_acc = stack.enter_context(tc.psum_pool(name="psum_acc", bufs=3))
        psum_back = stack.enter_context(tc.psum_pool(name="psum_back", bufs=3))

        x_chunks = []
        for c in range(CHUNKS):
            x_chunk = x_pool.tile([P, CHUNK_TILES, D], BF16)
            x_chunks.append(x_chunk)

        def load_x(c, tiles_a_load):
            for j in range(0, CHUNK_TILES, tiles_a_load):
                first = c * CHUNK_TILES + j
                nc.sync.dma_start(
                    out=x_chunks[c][:, j : j + tiles_a_load, :], in_=x_rows[:, first : first + tiles_a_load, :]
                )

        b_rows = const.tile([BLOCKS, P], BF16)
        nc.sync.dma_start(out=b_rows[:], in_=b1.rearrange("(b f) -> b f", f=P))
        load_x(0, 1)
        load_x(1, CHUNK_TILES)

        w_codes = const.tile([P, E], U32, align_bytes=64)
        nc.sync.dma_start(
            out=w_codes[:].bitcast(I32),
            in_=W1_words[0].rearrange("p n t -> p (n t)").bitcast(I32),
        )
        gain = const.tile([P, PACK], BF16)
        nc.sync.dma_start(out=gain[:], in_=g.rearrange("(q t) -> q t", t=PACK))
        w_scales = const.tile([P, E], U8, align_bytes=64)
        nc.vector.memset(w_scales[:].bitcast(I32), 0)
        for quadrant in range(4):
            nc.sync.dma_start(
                out=w_scales[32 * quadrant : 32 * quadrant + 4, :].bitcast(I32),
                in_=W1_scales[0, 4 * quadrant : 4 * quadrant + 4, :].bitcast(I32),
            )
        for c in range(2, CHUNKS):
            load_x(c, CHUNK_TILES)

        ident = const.tile([P, P], F32)
        make_identity(nc, ident[:])
        eps_rms = const.tile([P, 1], F32)
        nc.vector.memset(eps_rms[:], EPS_RMS)
        plus_floor = const.tile([P, 1], F32)
        nc.vector.memset(plus_floor[:], EPS_NORM * EPS_NORM)
        minus_floor = const.tile([P, 1], F32)
        nc.vector.memset(minus_floor[:], -EPS_NORM * EPS_NORM)
        table_warm = const.tile([P, 1], F32)
        nc.scalar.activation(out=table_warm[:], in_=eps_rms[:], func=ACT.Abs_reciprocal_sqrt)

        b_square = const.tile([P, P], F32)
        nc.vector.memset(b_square[:], 0.0)
        nc.vector.tensor_copy(out=b_square[0:BLOCKS, :], in_=b_rows[:])
        b_turned = psum_front.tile([P, PACK, P], F32, tag="turned")
        nc.tensor.transpose(out=b_turned[:, 0, :], in_=b_square[:], identity=ident[:])
        bias = const.tile([P, BLOCKS], F32)
        nc.vector.tensor_copy(out=bias[:], in_=b_turned[:, 0, 0:BLOCKS])

        square_junk = const.tile([P, D], BF16)
        assist_junk = const.tile([P, D], F32)

        sumsq, rms, rstd = {}, {}, {}
        scaled, turned, grouped = {}, {}, {}
        codes, scales = {}, {}
        acc, relu = {}, {}
        right, sumsq_right, norm, inv_norm = {}, {}, {}, {}

        def sum_squares(m):
            c, j = divmod(m, CHUNK_TILES)
            if j == 0:
                sumsq_tile = stat_pool.tile([P, CHUNK_TILES], F32)
                sumsq[c] = sumsq_tile
            if m < ASSISTED_TILES and m % 2 == 1:
                nc.vector.scalar_tensor_tensor(
                    out=assist_junk[:],
                    in0=x_chunks[c][:, j, :],
                    scalar=1.0,
                    in1=x_chunks[c][:, j, :],
                    op0=ALU.mult,
                    op1=ALU.mult,
                    accum_out=sumsq[c][:, j : j + 1],
                )
            else:
                nc.scalar.activation(
                    out=square_junk[:], in_=x_chunks[c][:, j, :], func=ACT.Square, accum_out=sumsq[c][:, j : j + 1]
                )

        def root_rms(m):
            c, j = divmod(m, CHUNK_TILES)
            if j == 0:
                rstd_tile = stat_pool.tile([P, CHUNK_TILES], F32)
                rstd[c] = rstd_tile
            if c == 0:
                tiles = slice(j, j + 1)
            elif j == CHUNK_TILES - 1:
                tiles = slice(0, CHUNK_TILES)
            else:
                return
            nc.scalar.activation(
                out=rstd[c][:, tiles],
                in_=sumsq[c][:, tiles],
                func=ACT.Abs_reciprocal_sqrt,
                bias=eps_rms[:],
                scale=1.0 / D,
            )

        def scale_tile(m):
            c, j = divmod(m, CHUNK_TILES)
            scaled_tile = tile_pool.tile([P, PACK, P], F32)
            scaled[m] = scaled_tile
            nc.gpsimd.tensor_scalar(
                out=scaled_tile[:],
                in0=x_chunks[c][:, j, :].rearrange("p (q t) -> p t q", t=PACK),
                scalar1=rstd[c][:, j : j + 1],
                scalar2=0.0,
                op0=ALU.mult,
                op1=ALU.add,
            )

        def turn_tile(m):
            turned_tile = psum_front.tile([P, PACK, P], F32, tag="turned")
            turned[m] = turned_tile
            for t in range(PACK):
                nc.tensor.transpose(out=turned_tile[:, t, :], in_=scaled[m][:, t, :], identity=ident[:])

        def gain_tile(m):
            c, j = divmod(m, CHUNK_TILES)
            if j == 0:
                grouped_tile = tile_pool.tile([P, CHUNK_TILES, P, PACK], BF16, align_bytes=64)
                grouped[c] = grouped_tile
            nc.vector.tensor_tensor(
                out=grouped[c][:, j, :, :],
                in0=turned[m][:].rearrange("q t r -> q r t"),
                in1=gain[:].unsqueeze(1).to_broadcast([P, P, PACK]),
                op=ALU.mult,
            )

        def quantise_tile(m):
            c, j = divmod(m, CHUNK_TILES)
            if j == CHUNK_TILES - 1:
                codes_tile = code_pool.tile([P, CHUNK], U32, align_bytes=64)
                scales_tile = code_pool.tile([P, CHUNK], U8, align_bytes=64)
                codes[c] = codes_tile
                scales[c] = scales_tile
                nc.vector.quantize_mx(
                    out=codes_tile[:].bitcast(FP8X4),
                    scales=scales_tile[:],
                    in_=grouped[c][:].rearrange("q j r t -> q (j r t)"),
                )

        def quarter_of(v):
            return (v + RIGHT) % QUARTERS

        def multiply(s):
            c, v = divmod(s, QUARTERS)
            for b in range(RUN):
                block = quarter_of(v) * RUN + b
                features = slice(block * P, (block + 1) * P)
                acc_tile = psum_acc.tile([P, CHUNK], F32)
                acc[s, b] = acc_tile
                nc.tensor.matmul_mx(
                    out=acc_tile[:],
                    lhsT=w_codes[:, features].bitcast(FP8X4),
                    lhsT_scale=w_scales[:, features],
                    rhs=codes[c][:].bitcast(FP8X4),
                    rhs_scale=scales[c][:],
                    start=True,
                    stop=True,
                )

        def bias_relu(s, b):
            v = s % QUARTERS
            if b == 0:
                relu_tile = relu_pool.tile([P, RUN, CHUNK], F32)
                relu[s] = relu_tile
            block = quarter_of(v) * RUN + b
            nc.vector.tensor_scalar(
                out=relu[s][:, b, :],
                in0=acc[s, b][:],
                scalar1=bias[:, block : block + 1],
                scalar2=0.0,
                op0=ALU.add,
                op1=ALU.max,
            )

        def store_pair(c, quarter, tile, first):
            rows = slice(c * CHUNK_TILES + first, c * CHUNK_TILES + first + BANK_TILES)
            nc.sync.dma_start(out=quarter_rows[quarter][:, rows, :], in_=tile[:, first : first + BANK_TILES, :])

        def turn_back_and_square(s):
            c, v = divmod(s, QUARTERS)
            squared = out_pool.tile([P, CHUNK_TILES, WIDTH], F32)
            for first in range(0, CHUNK_TILES, BANK_TILES):
                back = psum_back.tile([P, BANK_TILES, RUN, P], F32)
                for i in range(BANK_TILES):
                    tokens = slice((first + i) * P, (first + i + 1) * P)
                    for b in range(RUN):
                        nc.tensor.transpose(out=back[:, i, b, :], in_=relu[s][:, b, tokens], identity=ident[:])
                nc.scalar.activation(
                    out=squared[:, first : first + BANK_TILES, :],
                    in_=back[:].rearrange("r i b f -> r i (b f)"),
                    func=ACT.Square,
                )
                if quarter_of(v) != RIGHT:
                    store_pair(c, quarter_of(v), squared, first)
                if first == 0:
                    invert_norm(s)
            if quarter_of(v) == RIGHT:
                right[c] = squared

        def sum_squares_right(s):
            c, v = divmod(s, QUARTERS)
            if v == 0:
                sumsq_right_tile = stat_pool.tile([P, CHUNK_TILES], F32)
                sumsq_right[c] = sumsq_right_tile
            if v < 2:
                for j in range(2 * v, 2 * v + 2):
                    nc.scalar.activation(
                        out=square_junk[:, 0:WIDTH],
                        in_=right[c][:, j, :],
                        func=ACT.Square,
                        accum_out=sumsq_right[c][:, j : j + 1],
                    )

        def clamp_norm(s):
            c, v = divmod(s, QUARTERS)
            if v == 2:
                norm_tile = stat_pool.tile([P, CHUNK_TILES], F32)
                norm[c] = norm_tile
                nc.scalar.activation(out=norm_tile[:], in_=sumsq_right[c][:], func=ACT.Relu, bias=minus_floor[:])

        def invert_norm(s):
            c, v = divmod(s, QUARTERS)
            if v == 2:
                inv_norm_tile = stat_pool.tile([P, CHUNK_TILES], F32)
                inv_norm[c] = inv_norm_tile
                nc.scalar.activation(
                    out=inv_norm_tile[:], in_=norm[c][:], func=ACT.Abs_reciprocal_sqrt, bias=plus_floor[:]
                )

        def normalise_right(s):
            c, v = divmod(s, QUARTERS)
            if v >= 2:
                for j in range(2 * (v - 2), 2 * (v - 2) + 2):
                    nc.gpsimd.tensor_scalar(
                        out=right[c][:, j, :],
                        in0=right[c][:, j, :],
                        scalar1=inv_norm[c][:, j : j + 1],
                        scalar2=0.0,
                        op0=ALU.mult,
                        op1=ALU.add,
                    )
                store_pair(c, RIGHT, right[c], 2 * (v - 2))

        def run(stage, index, count):
            if 0 <= index < count:
                stage(index)

        for k in range(-LEAD_SUMSQ, STEPS - LEAD_SQUARE):
            run(sum_squares, k + LEAD_SUMSQ, TILES)
            run(root_rms, k + LEAD_SUMSQ - 1, TILES)
            run(clamp_norm, k + LEAD_SQUARE, STEPS)
            run(lambda s: bias_relu(s, 0), k, STEPS)
            run(lambda s: bias_relu(s, 1), k, STEPS)
            run(turn_back_and_square, k + LEAD_SQUARE, STEPS)
            run(multiply, k + LEAD_MULTIPLY, STEPS)
            run(turn_tile, k + LEAD_TURN, TILES)
            run(gain_tile, k + LEAD_GAIN, TILES)
            run(quantise_tile, k + LEAD_QUANTISE, TILES)
            run(sum_squares_right, k + LEAD_SQUARE, STEPS)
            run(scale_tile, k + LEAD_SCALE, TILES)
            run(normalise_right, k + LEAD_SQUARE, STEPS)
